import numpy as np
import ml_dtypes

BF16 = ml_dtypes.bfloat16


def bf(x):
    return np.asarray(x, np.float32).astype(BF16)


def f32(x):
    return np.asarray(x, np.float32)


def f64(x):
    return np.asarray(x).astype(np.float64)


def striped(idx):
    return np.tile(idx.reshape(-1, 16).T, (8, 1))


D, S, B, T, N = 256, 4096, 2, 1024, 2048
EPS = 1e-6


def setup_inputs():
    return {"q": f32(np.random.standard_normal((D, N))), "k": f32(np.random.standard_normal((D, N))), "v": f32(np.random.standard_normal((D, N))), "emb": f32(np.random.standard_normal((D, S))), "offs": striped(np.random.permutation(S)[:N])}


def reference(q, k, v, emb, offs):
    idx = offs[:16].T.reshape(-1)
    e = f64(emb)[:, idx]
    qe = e + f64(q)
    ke = e + f64(k)
    ve = e + f64(v)
    res = np.zeros((D, N))
    for b in range(B):
        cols = slice(b * T, (b + 1) * T)
        sc = qe[:, cols].T @ ke[:, cols] / np.sqrt(D)
        mu = sc.sum(axis=1, keepdims=True) / T
        sd = np.sqrt(((sc - mu) ** 2).sum(axis=1, keepdims=True) / (T - 1))
        z = (sc - mu) / (sd + EPS)
        p = np.exp(z - z.max(axis=1, keepdims=True))
        p = p / p.sum(axis=1, keepdims=True)
        res[:, cols] = ve[:, cols] @ p.T
    return res

@@ -1,0 +1,186 @@
+import concourse.mybir as mybir
+from concourse.masks import make_identity
+
+F32, BF16, U16 = mybir.dt.float32, mybir.dt.bfloat16, mybir.dt.uint16
+ADD, MULT, MAX = mybir.AluOpType.add, mybir.AluOpType.mult, mybir.AluOpType.max
+FUNC = mybir.ActivationFunctionType
+
+P = 128
+CHANNELS, TABLE_COLS, SAMPLES, TOKENS = 256, 4096, 2, 1024
+CB = CHANNELS // P
+TB = TOKENS // P
+BANK = 512
+HALVES = TOKENS // BANK
+GROUP = BANK // P
+LIST_COLS = TOKENS // 16
+EPS = 1e-6
+SCALE = 16.0
+LN_FLOOR = 2.0**-64
+
+FLOPS = 2 * 2 * SAMPLES * TOKENS * TOKENS * CHANNELS
+
+
+def tile_neuromodulatedattentionwithelectrodes_b_kernel(tc, q, k, v, emb, offs, out):
+    nc = tc.nc
+    with (
+        tc.tile_pool(name="held", bufs=1) as held,
+        tc.tile_pool(name="stats", bufs=4) as stats,
+        tc.tile_pool(name="rows", bufs=3) as rows,
+        tc.tile_pool(name="flipped", bufs=2) as flipped,
+        tc.tile_pool(name="staged", bufs=2) as staged,
+        tc.psum_pool(name="score_banks", bufs=4) as score_banks,
+        tc.psum_pool(name="flip_banks", bufs=2) as flip_banks,
+        tc.psum_pool(name="wide_banks", bufs=2) as wide_banks,
+    ):
+        ident32 = held.tile([P, P], F32, name="ident32")
+        make_identity(nc, ident32[:])
+        ident16 = held.tile([P, P], BF16, name="ident16")
+        make_identity(nc, ident16[:])
+
+        offsets = held.tile([P, SAMPLES * LIST_COLS], U16, name="offsets")
+        nc.sync.dma_start(offsets[:], offs)
+        table = [held.tile([P, TABLE_COLS], F32, name="table%d" % c) for c in range(CB)]
+        sources = {"q": q, "k": k, "v": v}
+        plain = {}
+
+        def load(name, c, s):
+            plain[name, c, s] = held.tile([P, TOKENS], F32, name="%s_plain%d%d" % (name, c, s))
+            nc.sync.dma_start(
+                plain[name, c, s][:], sources[name][c * P : (c + 1) * P, s * TOKENS : (s + 1) * TOKENS]
+            )
+
+        for c in range(CB):
+            nc.sync.dma_start(table[c][:], emb[c * P : (c + 1) * P, :])
+            load("k", c, 0)
+            load("q", c, 0)
+        for name, s in (("v", 0), ("k", 1), ("q", 1), ("v", 1)):
+            for c in range(CB):
+                load(name, c, s)
+
+        summed = {}
+        rounded = {}
+
+        def add_embedding(name, c, s):
+            summed[name, c, s] = held.tile([P, TOKENS], F32, name="%s_sum%d%d" % (name, c, s))
+            nc.vector.tensor_tensor(
+                summed[name, c, s][:],
+                table[c][:].indirect(offsets[:, s * LIST_COLS : (s + 1) * LIST_COLS]),
+                plain[name, c, s][:],
+                ADD,
+            )
+            if name != "v":
+                rounded[name, c, s] = held.tile([P, TOKENS], BF16, name="%s_bf%d%d" % (name, c, s))
+                nc.scalar.copy(rounded[name, c, s][:], summed[name, c, s][:])
+
+        values = {}
+
+        def flip_values(s):
+            values[s] = held.tile([P, TB, CHANNELS], BF16, name="values%d" % s)
+            for pair in range(TB // 2):
+                bank = wide_banks.tile([P, 2, CHANNELS], F32, name="bank", tag="wide")
+                for t in range(2):
+                    tb = 2 * pair + t
+                    for c in range(CB):
+                        nc.tensor.transpose(
+                            bank[:, t, c * P : (c + 1) * P], summed["v", c, s][:, tb * P : (tb + 1) * P], ident32[:]
+                        )
+                nc.scalar.copy(values[s][:, 2 * pair : 2 * pair + 2, :], bank[:])
+
+        def softmax_rows(s, jb):
+            score = []
+            for h in range(HALVES):
+                score.append(score_banks.tile([P, BANK], F32, name="score"))
+                for c in range(CB):
+                    nc.tensor.matmul(
+                        score[h][:],
+                        lhsT=rounded["q", c, s][:, jb * P : (jb + 1) * P],
+                        rhs=rounded["k", c, s][:, h * BANK : (h + 1) * BANK],
+                        start=(c == 0),
+                        stop=(c == CB - 1),
+                    )
+            parts = stats.tile([P, HALVES, 6], F32, name="parts")
+            for h in range(HALVES):
+                nc.vector.bn_stats(parts[:, h, :], score[h][:])
+            mean_var = stats.tile([P, 2], F32, name="mean_var")
+            nc.vector.bn_aggr(mean_var[:], parts[:].rearrange("p h x -> p (h x)"))
+            variance = stats.tile([P, 1], F32, name="variance")
+            nc.vector.tensor_scalar(variance[:], mean_var[:, 1:2], TOKENS / (TOKENS - 1.0), LN_FLOOR, MULT, MAX)
+            log_var = stats.tile([P, 1], F32, name="log_var")
+            nc.scalar.activation(log_var[:], variance[:], FUNC.Ln)
+            deviation = stats.tile([P, 1], F32, name="deviation")
+            nc.scalar.activation(deviation[:], log_var[:], FUNC.Exp, scale=0.5)
+            padded = stats.tile([P, 1], F32, name="padded")
+            nc.vector.tensor_scalar(padded[:], deviation[:], SCALE * EPS, None, ADD)
+            gain = stats.tile([P, 1], F32, name="gain")
+            nc.vector.reciprocal(gain[:], padded[:])
+            shift = stats.tile([P, 1], F32, name="shift")
+            nc.vector.scalar_tensor_tensor(shift[:], mean_var[:, 0:1], -1.0, gain[:], MULT, MULT)
+            weights = rows.tile([P, TOKENS], BF16, name="weights")
+            sums = stats.tile([P, HALVES], F32, name="sums")
+            for h in range(HALVES):
+                nc.scalar.activation(
+                    weights[:, h * BANK : (h + 1) * BANK],
+                    score[h][:],
+                    FUNC.Exp,
+                    bias=shift[:],
+                    scale=gain[:],
+                    accum_out=sums[:, h : h + 1],
+                )
+            return weights, sums
+
+        def flip_rows(weights, sums, group, jq):
+            total = stats.tile([P, 1], F32, name="total")
+            nc.vector.tensor_tensor(total[:], sums[:, 0:1], sums[:, 1:2], ADD)
+            inverse = stats.tile([P, 1], F32, name="inverse")
+            nc.vector.reciprocal(inverse[:], total[:])
+            softmax = rows.tile([P, TOKENS], BF16, name="softmax")
+            nc.vector.tensor_scalar(softmax[:], weights[:], inverse[:], None, MULT)
+            bank = flip_banks.tile([P, TB, P], BF16, name="flip")
+            for tb in range(TB):
+                nc.tensor.transpose(bank[:, tb, :], softmax[:, tb * P : (tb + 1) * P], ident16[:])
+            nc.scalar.copy(group[:, :, jq * P : (jq + 1) * P], bank[:])
+
+        def attend(s, g, group):
+            for c in range(CB):
+                acc = wide_banks.tile([P, BANK], F32, name="acc", tag="wide")
+                for tb in range(TB):
+                    nc.tensor.matmul(
+                        acc[:],
+                        lhsT=values[s][:, tb, c * P : (c + 1) * P],
+                        rhs=group[:, tb, :],
+                        start=(tb == 0),
+                        stop=(tb == TB - 1),
+                    )
+                result = staged.tile([P, BANK], F32, name="result")
+                nc.scalar.copy(result[:], acc[:])
+                first = s * TOKENS + g * BANK
+                nc.sync.dma_start(out[c * P : (c + 1) * P, first : first + BANK], result[:])
+
+        for c in range(CB):
+            add_embedding("k", c, 0)
+            add_embedding("q", c, 0)
+        later = [("v", c, 0) for c in range(CB)] + [(name, c, 1) for name in ("k", "q", "v") for c in range(CB)]
+
+        keys_first = {}
+
+        def finish(s, jb, weights, sums):
+            g = jb // GROUP
+            if jb % GROUP == 0:
+                keys_first[s, g] = flipped.tile([P, TB, BANK], BF16, name="keys_first")
+            flip_rows(weights, sums, keys_first[s, g], jb % GROUP)
+            if jb % GROUP == GROUP - 1:
+                attend(s, g, keys_first[s, g])
+
+        waiting = None
+        for s in range(SAMPLES):
+            for jb in range(TB):
+                weights, sums = softmax_rows(s, jb)
+                if s == 0:
+                    name, c, s_later = later[jb]
+                    add_embedding(name, c, s_later)
+                    if name == "v" and c == CB - 1:
+                        flip_values(s_later)
+                if waiting is not None:
+                    finish(*waiting)
+                waiting = (s, jb, weights, sums)
+        finish(*waiting)

@@ -2,20 +2,21 @@ import concourse.mybir as mybir
 from concourse.masks import make_identity
 
 F32, BF16, U16 = mybir.dt.float32, mybir.dt.bfloat16, mybir.dt.uint16
-ADD, MULT, MAX = mybir.AluOpType.add, mybir.AluOpType.mult, mybir.AluOpType.max
+ADD, MULT, POW = mybir.AluOpType.add, mybir.AluOpType.mult, mybir.AluOpType.pow
 FUNC = mybir.ActivationFunctionType
 
 P = 128
 CHANNELS, TABLE_COLS, SAMPLES, TOKENS = 256, 4096, 2, 1024
 CB = CHANNELS // P
 TB = TOKENS // P
+BLOCKS = SAMPLES * TB
 BANK = 512
 HALVES = TOKENS // BANK
 GROUP = BANK // P
-LIST_COLS = TOKENS // 16
 EPS = 1e-6
 SCALE = 16.0
-LN_FLOOR = 2.0**-64
+UNBIAS = (TOKENS / (TOKENS - 1.0)) ** 0.5
+LAG = 2
 
 FLOPS = 2 * 2 * SAMPLES * TOKENS * TOKENS * CHANNELS
 
@@ -25,7 +26,7 @@ def tile_neuromodulatedattentionwithelectrodes_b_kernel(tc, q, k, v, emb, offs, 
     with (
         tc.tile_pool(name="held", bufs=1) as held,
         tc.tile_pool(name="stats", bufs=4) as stats,
-        tc.tile_pool(name="rows", bufs=3) as rows,
+        tc.tile_pool(name="rows", bufs=4) as rows,
         tc.tile_pool(name="flipped", bufs=2) as flipped,
         tc.tile_pool(name="staged", bufs=2) as staged,
         tc.psum_pool(name="score_banks", bufs=4) as score_banks,
@@ -36,8 +37,10 @@ def tile_neuromodulatedattentionwithelectrodes_b_kernel(tc, q, k, v, emb, offs, 
         make_identity(nc, ident32[:])
         ident16 = held.tile([P, P], BF16, name="ident16")
         make_identity(nc, ident16[:])
+        half = held.tile([P, 1], F32, name="half")
+        nc.gpsimd.memset(half[:], 0.5)
 
-        offsets = held.tile([P, SAMPLES * LIST_COLS], U16, name="offsets")
+        offsets = held.tile([P, SAMPLES * TOKENS // 16], U16, name="offsets")
         nc.sync.dma_start(offsets[:], offs)
         table = [held.tile([P, TABLE_COLS], F32, name="table%d" % c) for c in range(CB)]
         sources = {"q": q, "k": k, "v": v}
@@ -59,128 +62,135 @@ def tile_neuromodulatedattentionwithelectrodes_b_kernel(tc, q, k, v, emb, offs, 
 
         summed = {}
         rounded = {}
+        values = {}
 
-        def add_embedding(name, c, s):
-            summed[name, c, s] = held.tile([P, TOKENS], F32, name="%s_sum%d%d" % (name, c, s))
+        def add_embedding(name, c, s, h):
+            first = s * TOKENS + h * BANK
+            summed[name, c, s, h] = held.tile([P, BANK], F32, name="%s_sum%d%d%d" % (name, c, s, h))
             nc.vector.tensor_tensor(
-                summed[name, c, s][:],
-                table[c][:].indirect(offsets[:, s * LIST_COLS : (s + 1) * LIST_COLS]),
-                plain[name, c, s][:],
+                summed[name, c, s, h][:],
+                table[c][:].indirect(offsets[:, first // 16 : (first + BANK) // 16]),
+                plain[name, c, s][:, h * BANK : (h + 1) * BANK],
                 ADD,
             )
             if name != "v":
-                rounded[name, c, s] = held.tile([P, TOKENS], BF16, name="%s_bf%d%d" % (name, c, s))
-                nc.scalar.copy(rounded[name, c, s][:], summed[name, c, s][:])
+                rounded[name, c, s, h] = held.tile([P, BANK], BF16, name="%s_bf%d%d%d" % (name, c, s, h))
+                nc.scalar.copy(rounded[name, c, s, h][:], summed[name, c, s, h][:])
+            elif c == CB - 1:
+                flip_values(s, h)
 
-        values = {}
-
-        def flip_values(s):
-            values[s] = held.tile([P, TB, CHANNELS], BF16, name="values%d" % s)
-            for pair in range(TB // 2):
+        def flip_values(s, h):
+            values[s, h] = held.tile([P, GROUP, CHANNELS], BF16, name="values%d%d" % (s, h))
+            for pair in range(GROUP // 2):
                 bank = wide_banks.tile([P, 2, CHANNELS], F32, name="bank", tag="wide")
                 for t in range(2):
                     tb = 2 * pair + t
                     for c in range(CB):
                         nc.tensor.transpose(
-                            bank[:, t, c * P : (c + 1) * P], summed["v", c, s][:, tb * P : (tb + 1) * P], ident32[:]
+                            bank[:, t, c * P : (c + 1) * P], summed["v", c, s, h][:, tb * P : (tb + 1) * P], ident32[:]
                         )
-                nc.scalar.copy(values[s][:, 2 * pair : 2 * pair + 2, :], bank[:])
+                nc.scalar.copy(values[s, h][:, 2 * pair : 2 * pair + 2, :], bank[:])
 
-        def softmax_rows(s, jb):
-            score = []
+        score, mean_var, deviation, weights, sums = {}, {}, {}, {}, {}
+
+        def scores(i):
+            s, jb = divmod(i, TB)
             for h in range(HALVES):
-                score.append(score_banks.tile([P, BANK], F32, name="score"))
+                score[i, h] = score_banks.tile([P, BANK], F32, name="score")
                 for c in range(CB):
                     nc.tensor.matmul(
-                        score[h][:],
-                        lhsT=rounded["q", c, s][:, jb * P : (jb + 1) * P],
-                        rhs=rounded["k", c, s][:, h * BANK : (h + 1) * BANK],
+                        score[i, h][:],
+                        lhsT=rounded["q", c, s, jb // GROUP][:, (jb % GROUP) * P : (jb % GROUP + 1) * P],
+                        rhs=rounded["k", c, s, h][:],
                         start=(c == 0),
                         stop=(c == CB - 1),
                     )
+
+        def row_statistics(i):
             parts = stats.tile([P, HALVES, 6], F32, name="parts")
             for h in range(HALVES):
-                nc.vector.bn_stats(parts[:, h, :], score[h][:])
-            mean_var = stats.tile([P, 2], F32, name="mean_var")
-            nc.vector.bn_aggr(mean_var[:], parts[:].rearrange("p h x -> p (h x)"))
-            variance = stats.tile([P, 1], F32, name="variance")
-            nc.vector.tensor_scalar(variance[:], mean_var[:, 1:2], TOKENS / (TOKENS - 1.0), LN_FLOOR, MULT, MAX)
-            log_var = stats.tile([P, 1], F32, name="log_var")
-            nc.scalar.activation(log_var[:], variance[:], FUNC.Ln)
-            deviation = stats.tile([P, 1], F32, name="deviation")
-            nc.scalar.activation(deviation[:], log_var[:], FUNC.Exp, scale=0.5)
+                nc.vector.bn_stats(parts[:, h, :], score[i, h][:])
+            mean_var[i] = stats.tile([P, 2], F32, name="mean_var")
+            nc.vector.bn_aggr(mean_var[i][:], parts[:].rearrange("p h x -> p (h x)"))
+            deviation[i] = stats.tile([P, 1], F32, name="deviation")
+            nc.gpsimd.tensor_tensor(deviation[i][:], mean_var[i][:, 1:2], half[:], POW)
+
+        def exponentials(i):
             padded = stats.tile([P, 1], F32, name="padded")
-            nc.vector.tensor_scalar(padded[:], deviation[:], SCALE * EPS, None, ADD)
+            nc.vector.tensor_scalar(padded[:], deviation[i][:], UNBIAS, SCALE * EPS, MULT, ADD)
             gain = stats.tile([P, 1], F32, name="gain")
             nc.vector.reciprocal(gain[:], padded[:])
             shift = stats.tile([P, 1], F32, name="shift")
-            nc.vector.scalar_tensor_tensor(shift[:], mean_var[:, 0:1], -1.0, gain[:], MULT, MULT)
-            weights = rows.tile([P, TOKENS], BF16, name="weights")
-            sums = stats.tile([P, HALVES], F32, name="sums")
+            nc.vector.scalar_tensor_tensor(shift[:], mean_var[i][:, 0:1], -1.0, gain[:], MULT, MULT)
+            weights[i] = rows.tile([P, TOKENS], BF16, name="weights")
+            sums[i] = stats.tile([P, HALVES], F32, name="sums")
             for h in range(HALVES):
                 nc.scalar.activation(
-                    weights[:, h * BANK : (h + 1) * BANK],
-                    score[h][:],
+                    weights[i][:, h * BANK : (h + 1) * BANK],
+                    score[i, h][:],
                     FUNC.Exp,
                     bias=shift[:],
                     scale=gain[:],
-                    accum_out=sums[:, h : h + 1],
+                    accum_out=sums[i][:, h : h + 1],
                 )
-            return weights, sums
-
-        def flip_rows(weights, sums, group, jq):
-            total = stats.tile([P, 1], F32, name="total")
-            nc.vector.tensor_tensor(total[:], sums[:, 0:1], sums[:, 1:2], ADD)
-            inverse = stats.tile([P, 1], F32, name="inverse")
-            nc.vector.reciprocal(inverse[:], total[:])
-            softmax = rows.tile([P, TOKENS], BF16, name="softmax")
-            nc.vector.tensor_scalar(softmax[:], weights[:], inverse[:], None, MULT)
-            bank = flip_banks.tile([P, TB, P], BF16, name="flip")
-            for tb in range(TB):
-                nc.tensor.transpose(bank[:, tb, :], softmax[:, tb * P : (tb + 1) * P], ident16[:])
-            nc.scalar.copy(group[:, :, jq * P : (jq + 1) * P], bank[:])
-
-        def attend(s, g, group):
-            for c in range(CB):
-                acc = wide_banks.tile([P, BANK], F32, name="acc", tag="wide")
-                for tb in range(TB):
-                    nc.tensor.matmul(
-                        acc[:],
-                        lhsT=values[s][:, tb, c * P : (c + 1) * P],
-                        rhs=group[:, tb, :],
-                        start=(tb == 0),
-                        stop=(tb == TB - 1),
-                    )
-                result = staged.tile([P, BANK], F32, name="result")
-                nc.scalar.copy(result[:], acc[:])
-                first = s * TOKENS + g * BANK
-                nc.sync.dma_start(out[c * P : (c + 1) * P, first : first + BANK], result[:])
-
-        for c in range(CB):
-            add_embedding("k", c, 0)
-            add_embedding("q", c, 0)
-        later = [("v", c, 0) for c in range(CB)] + [(name, c, 1) for name in ("k", "q", "v") for c in range(CB)]
 
         keys_first = {}
 
-        def finish(s, jb, weights, sums):
-            g = jb // GROUP
-            if jb % GROUP == 0:
-                keys_first[s, g] = flipped.tile([P, TB, BANK], BF16, name="keys_first")
-            flip_rows(weights, sums, keys_first[s, g], jb % GROUP)
-            if jb % GROUP == GROUP - 1:
-                attend(s, g, keys_first[s, g])
+        def flip_rows(i):
+            total = stats.tile([P, 1], F32, name="total")
+            nc.vector.tensor_tensor(total[:], sums[i][:, 0:1], sums[i][:, 1:2], ADD)
+            inverse = stats.tile([P, 1], F32, name="inverse")
+            nc.vector.reciprocal(inverse[:], total[:])
+            softmax = rows.tile([P, TOKENS], BF16, name="softmax")
+            nc.vector.tensor_scalar(softmax[:], weights[i][:], inverse[:], None, MULT)
+            bank = flip_banks.tile([P, TB, P], BF16, name="flip")
+            for tb in range(TB):
+                nc.tensor.transpose(bank[:, tb, :], softmax[:, tb * P : (tb + 1) * P], ident16[:])
+            g, jq = divmod(i, GROUP)
+            if jq == 0:
+                keys_first[g] = flipped.tile([P, TB, BANK], BF16, name="keys_first")
+            nc.scalar.copy(keys_first[g][:, :, jq * P : (jq + 1) * P], bank[:])
 
-        waiting = None
-        for s in range(SAMPLES):
-            for jb in range(TB):
-                weights, sums = softmax_rows(s, jb)
-                if s == 0:
-                    name, c, s_later = later[jb]
-                    add_embedding(name, c, s_later)
-                    if name == "v" and c == CB - 1:
-                        flip_values(s_later)
-                if waiting is not None:
-                    finish(*waiting)
-                waiting = (s, jb, weights, sums)
-        finish(*waiting)
+        acc = {}
+
+        def attend(g, c, h):
+            s = g // HALVES
+            if h == 0:
+                acc[g, c] = wide_banks.tile([P, BANK], F32, name="acc", tag="wide")
+            for t in range(GROUP):
+                tb = h * GROUP + t
+                nc.tensor.matmul(
+                    acc[g, c][:],
+                    lhsT=values[s, h][:, t, c * P : (c + 1) * P],
+                    rhs=keys_first[g][:, tb, :],
+                    start=(tb == 0),
+                    stop=(tb == TB - 1),
+                )
+            if h == HALVES - 1:
+                result = staged.tile([P, BANK], F32, name="result")
+                nc.scalar.copy(result[:], acc[g, c][:])
+                nc.sync.dma_start(out[c * P : (c + 1) * P, g * BANK : (g + 1) * BANK], result[:])
+
+        def look_up(name, s, h):
+            for c in range(CB):
+                add_embedding(name, c, s, h)
+
+        for i in range(BLOCKS + LAG + GROUP):
+            s, jb = divmod(i, TB)
+            if i < BLOCKS:
+                if jb == 0:
+                    for h in range(HALVES):
+                        look_up("k", s, h)
+                if jb % GROUP == 0:
+                    look_up("q", s, jb // GROUP)
+                scores(i)
+            if i >= LAG + GROUP:
+                g, quarter = divmod(i - LAG - GROUP, GROUP)
+                if g % HALVES == 0 and quarter < HALVES:
+                    look_up("v", g // HALVES, quarter)
+                attend(g, quarter // HALVES, quarter % HALVES)
+            if LAG <= i < BLOCKS + LAG:
+                flip_rows(i - LAG)
+            if i < BLOCKS:
+                row_statistics(i)
+                exponentials(i)

@@ -97,7 +97,8 @@ def tile_neuromodulatedattentionwithelectrodes_b_kernel(tc, q, k, v, emb, offs, 
             s, jb = divmod(i, TB)
             for h in range(HALVES):
                 score[i, h] = score_banks.tile([P, BANK], F32, name="score")
-                for c in range(CB):
+            for c in range(CB):
+                for h in range(HALVES):
                     nc.tensor.matmul(
                         score[i, h][:],
                         lhsT=rounded["q", c, s, jb // GROUP][:, (jb % GROUP) * P : (jb % GROUP + 1) * P],

@@ -12,11 +12,14 @@ TB = TOKENS // P
 BLOCKS = SAMPLES * TB
 BANK = 512
 HALVES = TOKENS // BANK
-GROUP = BANK // P
+PER_BANK = BANK // P
+BN_STATS_DIM = 6
 EPS = 1e-6
 SCALE = 16.0
 UNBIAS = (TOKENS / (TOKENS - 1.0)) ** 0.5
 LAG = 2
+
+assert CB * HALVES == PER_BANK
 
 FLOPS = 2 * 2 * SAMPLES * TOKENS * TOKENS * CHANNELS
 
@@ -80,8 +83,8 @@ def tile_neuromodulatedattentionwithelectrodes_b_kernel(tc, q, k, v, emb, offs, 
                 flip_values(s, h)
 
         def flip_values(s, h):
-            values[s, h] = held.tile([P, GROUP, CHANNELS], BF16, name="values%d%d" % (s, h))
-            for pair in range(GROUP // 2):
+            values[s, h] = held.tile([P, PER_BANK, CHANNELS], BF16, name="values%d%d" % (s, h))
+            for pair in range(PER_BANK // 2):
                 bank = wide_banks.tile([P, 2, CHANNELS], F32, name="bank", tag="wide")
                 for t in range(2):
                     tb = 2 * pair + t
@@ -101,14 +104,14 @@ def tile_neuromodulatedattentionwithelectrodes_b_kernel(tc, q, k, v, emb, offs, 
                 for h in range(HALVES):
                     nc.tensor.matmul(
                         score[i, h][:],
-                        lhsT=rounded["q", c, s, jb // GROUP][:, (jb % GROUP) * P : (jb % GROUP + 1) * P],
+                        lhsT=rounded["q", c, s, jb // PER_BANK][:, (jb % PER_BANK) * P : (jb % PER_BANK + 1) * P],
                         rhs=rounded["k", c, s, h][:],
                         start=(c == 0),
                         stop=(c == CB - 1),
                     )
 
         def row_statistics(i):
-            parts = stats.tile([P, HALVES, 6], F32, name="parts")
+            parts = stats.tile([P, HALVES, BN_STATS_DIM], F32, name="parts")
             for h in range(HALVES):
                 nc.vector.bn_stats(parts[:, h, :], score[i, h][:])
             mean_var[i] = stats.tile([P, 2], F32, name="mean_var")
@@ -147,27 +150,27 @@ def tile_neuromodulatedattentionwithelectrodes_b_kernel(tc, q, k, v, emb, offs, 
             bank = flip_banks.tile([P, TB, P], BF16, name="flip")
             for tb in range(TB):
                 nc.tensor.transpose(bank[:, tb, :], softmax[:, tb * P : (tb + 1) * P], ident16[:])
-            g, jq = divmod(i, GROUP)
+            g, jq = divmod(i, PER_BANK)
             if jq == 0:
                 keys_first[g] = flipped.tile([P, TB, BANK], BF16, name="keys_first")
             nc.scalar.copy(keys_first[g][:, :, jq * P : (jq + 1) * P], bank[:])
 
         acc = {}
 
-        def attend(g, c, h):
+        def attend(g, c, h, first=0, count=PER_BANK):
             s = g // HALVES
-            if h == 0:
+            if h == 0 and first == 0:
                 acc[g, c] = wide_banks.tile([P, BANK], F32, name="acc", tag="wide")
-            for t in range(GROUP):
-                tb = h * GROUP + t
+            for t in range(PER_BANK):
+                tb = h * PER_BANK + t
                 nc.tensor.matmul(
-                    acc[g, c][:],
+                    acc[g, c][:, first * P : (first + count) * P],
                     lhsT=values[s, h][:, t, c * P : (c + 1) * P],
-                    rhs=keys_first[g][:, tb, :],
+                    rhs=keys_first[g][:, tb, first * P : (first + count) * P],
                     start=(tb == 0),
                     stop=(tb == TB - 1),
                 )
-            if h == HALVES - 1:
+            if h == HALVES - 1 and first + count == PER_BANK:
                 result = staged.tile([P, BANK], F32, name="result")
                 nc.scalar.copy(result[:], acc[g, c][:])
                 nc.sync.dma_start(out[c * P : (c + 1) * P, g * BANK : (g + 1) * BANK], result[:])
@@ -176,22 +179,30 @@ def tile_neuromodulatedattentionwithelectrodes_b_kernel(tc, q, k, v, emb, offs, 
             for c in range(CB):
                 add_embedding(name, c, s, h)
 
-        for i in range(BLOCKS + LAG + GROUP):
+        last_group = BLOCKS // PER_BANK - 1
+        for i in range(BLOCKS + LAG):
             s, jb = divmod(i, TB)
             if i < BLOCKS:
                 if jb == 0:
                     for h in range(HALVES):
                         look_up("k", s, h)
-                if jb % GROUP == 0:
-                    look_up("q", s, jb // GROUP)
+                if jb % PER_BANK == 0:
+                    look_up("q", s, jb // PER_BANK)
                 scores(i)
-            if i >= LAG + GROUP:
-                g, quarter = divmod(i - LAG - GROUP, GROUP)
+            if i >= LAG + PER_BANK:
+                g, quarter = divmod(i - LAG - PER_BANK, PER_BANK)
                 if g % HALVES == 0 and quarter < HALVES:
                     look_up("v", g // HALVES, quarter)
                 attend(g, quarter // HALVES, quarter % HALVES)
-            if LAG <= i < BLOCKS + LAG:
+            if i == BLOCKS + LAG - 1:
+                for c in range(CB):
+                    for h in range(HALVES):
+                        attend(last_group, c, h, 0, PER_BANK - 1)
+            if i >= LAG:
                 flip_rows(i - LAG)
             if i < BLOCKS:
                 row_statistics(i)
                 exponentials(i)
+        for c in range(CB):
+            for h in range(HALVES):
+                attend(last_group, c, h, PER_BANK - 1, 1)

@@ -13,6 +13,8 @@ BLOCKS = SAMPLES * TB
 BANK = 512
 HALVES = TOKENS // BANK
 PER_BANK = BANK // P
+PAIR = 2
+WB = TB // PAIR
 BN_STATS_DIM = 6
 EPS = 1e-6
 SCALE = 16.0
@@ -38,8 +40,6 @@ def tile_neuromodulatedattentionwithelectrodes_b_kernel(tc, q, k, v, emb, offs, 
     ):
         ident32 = held.tile([P, P], F32, name="ident32")
         make_identity(nc, ident32[:])
-        ident16 = held.tile([P, P], BF16, name="ident16")
-        make_identity(nc, ident16[:])
         half = held.tile([P, 1], F32, name="half")
         nc.gpsimd.memset(half[:], 0.5)
 
@@ -76,9 +76,15 @@ def tile_neuromodulatedattentionwithelectrodes_b_kernel(tc, q, k, v, emb, offs, 
                 plain[name, c, s][:, h * BANK : (h + 1) * BANK],
                 ADD,
             )
-            if name != "v":
+            if name == "q":
                 rounded[name, c, s, h] = held.tile([P, BANK], BF16, name="%s_bf%d%d%d" % (name, c, s, h))
                 nc.scalar.copy(rounded[name, c, s, h][:], summed[name, c, s, h][:])
+            elif name == "k":
+                rounded[name, c, s, h] = held.tile([P, BANK], BF16, name="%s_bf%d%d%d" % (name, c, s, h))
+                nc.scalar.copy(
+                    rounded[name, c, s, h][:].rearrange("p (b w e) -> p b w e", w=P, e=PAIR),
+                    summed[name, c, s, h][:].rearrange("p (b e w) -> p b w e", w=P, e=PAIR),
+                )
             elif c == CB - 1:
                 flip_values(s, h)
 
@@ -147,12 +153,13 @@ def tile_neuromodulatedattentionwithelectrodes_b_kernel(tc, q, k, v, emb, offs, 
             nc.vector.reciprocal(inverse[:], total[:])
             softmax = rows.tile([P, TOKENS], BF16, name="softmax")
             nc.vector.tensor_scalar(softmax[:], weights[i][:], inverse[:], None, MULT)
-            bank = flip_banks.tile([P, TB, P], BF16, name="flip")
-            for tb in range(TB):
-                nc.tensor.transpose(bank[:, tb, :], softmax[:, tb * P : (tb + 1) * P], ident16[:])
+            words = softmax[:].bitcast(F32)
+            bank = flip_banks.tile([P, WB, P], F32, name="flip")
+            for wb in range(WB):
+                nc.tensor.transpose(bank[:, wb, :], words[:, wb * P : (wb + 1) * P], ident32[:])
             g, jq = divmod(i, PER_BANK)
             if jq == 0:
-                keys_first[g] = flipped.tile([P, TB, BANK], BF16, name="keys_first")
+                keys_first[g] = flipped.tile([P, WB, BANK], F32, name="keys_first")
             nc.scalar.copy(keys_first[g][:, :, jq * P : (jq + 1) * P], bank[:])
 
         acc = {}
@@ -161,12 +168,14 @@ def tile_neuromodulatedattentionwithelectrodes_b_kernel(tc, q, k, v, emb, offs, 
             s = g // HALVES
             if h == 0 and first == 0:
                 acc[g, c] = wide_banks.tile([P, BANK], F32, name="acc", tag="wide")
+            halves = keys_first[g][:].rearrange("p b j -> p (b j)").bitcast(BF16)
+            halves = halves.rearrange("p (b j e) -> p b j e", b=WB, e=PAIR)
             for t in range(PER_BANK):
                 tb = h * PER_BANK + t
                 nc.tensor.matmul(
                     acc[g, c][:, first * P : (first + count) * P],
                     lhsT=values[s, h][:, t, c * P : (c + 1) * P],
-                    rhs=keys_first[g][:, tb, first * P : (first + count) * P],
+                    rhs=halves[:, tb // PAIR, first * P : (first + count) * P, tb % PAIR],
                     start=(tb == 0),
                     stop=(tb == TB - 1),
                 )

@@ -19,6 +19,7 @@ BN_STATS_DIM = 6
 EPS = 1e-6
 SCALE = 16.0
 UNBIAS = (TOKENS / (TOKENS - 1.0)) ** 0.5
+LAST_GROUP = BLOCKS // PER_BANK - 1
 LAG = 2
 
 assert CB * HALVES == PER_BANK
@@ -34,9 +35,8 @@ def tile_neuromodulatedattentionwithelectrodes_b_kernel(tc, q, k, v, emb, offs, 
         tc.tile_pool(name="rows", bufs=4) as rows,
         tc.tile_pool(name="flipped", bufs=2) as flipped,
         tc.tile_pool(name="staged", bufs=2) as staged,
-        tc.psum_pool(name="score_banks", bufs=4) as score_banks,
-        tc.psum_pool(name="flip_banks", bufs=2) as flip_banks,
-        tc.psum_pool(name="wide_banks", bufs=2) as wide_banks,
+        tc.psum_pool(name="score_banks", bufs=6) as score_banks,
+        tc.psum_pool(name="work_banks", bufs=2) as work_banks,
     ):
         ident32 = held.tile([P, P], F32, name="ident32")
         make_identity(nc, ident32[:])
@@ -91,7 +91,7 @@ def tile_neuromodulatedattentionwithelectrodes_b_kernel(tc, q, k, v, emb, offs, 
         def flip_values(s, h):
             values[s, h] = held.tile([P, PER_BANK, CHANNELS], BF16, name="values%d%d" % (s, h))
             for pair in range(PER_BANK // 2):
-                bank = wide_banks.tile([P, 2, CHANNELS], F32, name="bank", tag="wide")
+                bank = work_banks.tile([P, 2, CHANNELS], F32, name="bank", tag="work")
                 for t in range(2):
                     tb = 2 * pair + t
                     for c in range(CB):
@@ -154,7 +154,7 @@ def tile_neuromodulatedattentionwithelectrodes_b_kernel(tc, q, k, v, emb, offs, 
             softmax = rows.tile([P, TOKENS], BF16, name="softmax")
             nc.vector.tensor_scalar(softmax[:], weights[i][:], inverse[:], None, MULT)
             words = softmax[:].bitcast(F32)
-            bank = flip_banks.tile([P, WB, P], F32, name="flip")
+            bank = work_banks.tile([P, WB, P], F32, name="flip", tag="work")
             for wb in range(WB):
                 nc.tensor.transpose(bank[:, wb, :], words[:, wb * P : (wb + 1) * P], ident32[:])
             g, jq = divmod(i, PER_BANK)
@@ -167,7 +167,10 @@ def tile_neuromodulatedattentionwithelectrodes_b_kernel(tc, q, k, v, emb, offs, 
         def attend(g, c, h, first=0, count=PER_BANK):
             s = g // HALVES
             if h == 0 and first == 0:
-                acc[g, c] = wide_banks.tile([P, BANK], F32, name="acc", tag="wide")
+                if g < LAST_GROUP:
+                    acc[g, c] = work_banks.tile([P, BANK], F32, name="acc", tag="work")
+                else:
+                    acc[g, c] = score_banks.tile([P, BANK], F32, name="score")
             halves = keys_first[g][:].rearrange("p b j -> p (b j)").bitcast(BF16)
             halves = halves.rearrange("p (b j e) -> p b j e", b=WB, e=PAIR)
             for t in range(PER_BANK):
@@ -188,7 +191,6 @@ def tile_neuromodulatedattentionwithelectrodes_b_kernel(tc, q, k, v, emb, offs, 
             for c in range(CB):
                 add_embedding(name, c, s, h)
 
-        last_group = BLOCKS // PER_BANK - 1
         for i in range(BLOCKS + LAG):
             s, jb = divmod(i, TB)
             if i < BLOCKS:
@@ -206,7 +208,7 @@ def tile_neuromodulatedattentionwithelectrodes_b_kernel(tc, q, k, v, emb, offs, 
             if i == BLOCKS + LAG - 1:
                 for c in range(CB):
                     for h in range(HALVES):
-                        attend(last_group, c, h, 0, PER_BANK - 1)
+                        attend(LAST_GROUP, c, h, 0, PER_BANK - 1)
             if i >= LAG:
                 flip_rows(i - LAG)
             if i < BLOCKS:
@@ -214,4 +216,4 @@ def tile_neuromodulatedattentionwithelectrodes_b_kernel(tc, q, k, v, emb, offs, 
                 exponentials(i)
         for c in range(CB):
             for h in range(HALVES):
-                attend(last_group, c, h, PER_BANK - 1, 1)
+                attend(LAST_GROUP, c, h, PER_BANK - 1, 1)

@@ -14,12 +14,14 @@ BANK = 512
 HALVES = TOKENS // BANK
 PER_BANK = BANK // P
 PAIR = 2
+SHORT = PAIR * P
 WB = TB // PAIR
 BN_STATS_DIM = 6
 EPS = 1e-6
 SCALE = 16.0
 UNBIAS = (TOKENS / (TOKENS - 1.0)) ** 0.5
-LAST_GROUP = BLOCKS // PER_BANK - 1
+GROUPS = ((0, 4), (4, 4), (8, 4), (12, 3), (15, 1))
+WHOLE_GROUPS = 3
 LAG = 2
 
 assert CB * HALVES == PER_BANK
@@ -33,8 +35,8 @@ def tile_neuromodulatedattentionwithelectrodes_b_kernel(tc, q, k, v, emb, offs, 
         tc.tile_pool(name="held", bufs=1) as held,
         tc.tile_pool(name="stats", bufs=4) as stats,
         tc.tile_pool(name="rows", bufs=4) as rows,
-        tc.tile_pool(name="flipped", bufs=2) as flipped,
-        tc.tile_pool(name="staged", bufs=2) as staged,
+        tc.tile_pool(name="flipped", bufs=3) as flipped,
+        tc.tile_pool(name="staged", bufs=4) as staged,
         tc.psum_pool(name="score_banks", bufs=6) as score_banks,
         tc.psum_pool(name="work_banks", bufs=2) as work_banks,
     ):
@@ -49,43 +51,48 @@ def tile_neuromodulatedattentionwithelectrodes_b_kernel(tc, q, k, v, emb, offs, 
         sources = {"q": q, "k": k, "v": v}
         plain = {}
 
-        def load(name, c, s):
-            plain[name, c, s] = held.tile([P, TOKENS], F32, name="%s_plain%d%d" % (name, c, s))
-            nc.sync.dma_start(
-                plain[name, c, s][:], sources[name][c * P : (c + 1) * P, s * TOKENS : (s + 1) * TOKENS]
-            )
+        def load(name, c, s, pieces):
+            row = held.tile([P, len(pieces) * BANK], F32, name="%s_plain%d%d%d" % (name, c, s, pieces[0]))
+            first = s * TOKENS + pieces[0] * BANK
+            nc.sync.dma_start(row[:], sources[name][c * P : (c + 1) * P, first : first + len(pieces) * BANK])
+            for n, h in enumerate(pieces):
+                plain[name, c, s, h] = row[:, n * BANK : (n + 1) * BANK]
 
         for c in range(CB):
             nc.sync.dma_start(table[c][:], emb[c * P : (c + 1) * P, :])
-            load("k", c, 0)
-            load("q", c, 0)
+            load("k", c, 0, (0,))
+            load("k", c, 0, (1,))
+            load("q", c, 0, (0,))
+        for c in range(CB):
+            load("q", c, 0, (1,))
         for name, s in (("v", 0), ("k", 1), ("q", 1), ("v", 1)):
             for c in range(CB):
-                load(name, c, s)
+                load(name, c, s, (0, 1))
 
         summed = {}
         rounded = {}
         values = {}
 
         def add_embedding(name, c, s, h):
-            first = s * TOKENS + h * BANK
             summed[name, c, s, h] = held.tile([P, BANK], F32, name="%s_sum%d%d%d" % (name, c, s, h))
-            nc.vector.tensor_tensor(
-                summed[name, c, s, h][:],
-                table[c][:].indirect(offsets[:, first // 16 : (first + BANK) // 16]),
-                plain[name, c, s][:, h * BANK : (h + 1) * BANK],
-                ADD,
-            )
-            if name == "q":
+            if name != "v":
                 rounded[name, c, s, h] = held.tile([P, BANK], BF16, name="%s_bf%d%d%d" % (name, c, s, h))
-                nc.scalar.copy(rounded[name, c, s, h][:], summed[name, c, s, h][:])
-            elif name == "k":
-                rounded[name, c, s, h] = held.tile([P, BANK], BF16, name="%s_bf%d%d%d" % (name, c, s, h))
-                nc.scalar.copy(
-                    rounded[name, c, s, h][:].rearrange("p (b w e) -> p b w e", w=P, e=PAIR),
-                    summed[name, c, s, h][:].rearrange("p (b e w) -> p b w e", w=P, e=PAIR),
+            for n in range(0, BANK, SHORT):
+                first = s * TOKENS + h * BANK + n
+                nc.vector.tensor_tensor(
+                    summed[name, c, s, h][:, n : n + SHORT],
+                    table[c][:].indirect(offsets[:, first // 16 : (first + SHORT) // 16]),
+                    plain[name, c, s, h][:, n : n + SHORT],
+                    ADD,
                 )
-            elif c == CB - 1:
+                if name == "q":
+                    nc.scalar.copy(rounded[name, c, s, h][:, n : n + SHORT], summed[name, c, s, h][:, n : n + SHORT])
+                if name == "k":
+                    nc.scalar.copy(
+                        rounded[name, c, s, h][:, n : n + SHORT].rearrange("p (w e) -> p w e", e=PAIR),
+                        summed[name, c, s, h][:, n : n + SHORT].rearrange("p (e w) -> p w e", e=PAIR),
+                    )
+            if name == "v" and c == CB - 1:
                 flip_values(s, h)
 
         def flip_values(s, h):
@@ -145,6 +152,7 @@ def tile_neuromodulatedattentionwithelectrodes_b_kernel(tc, q, k, v, emb, offs, 
                 )
 
         keys_first = {}
+        place = {first + b: (g, b) for g, (first, count) in enumerate(GROUPS) for b in range(count)}
 
         def flip_rows(i):
             total = stats.tile([P, 1], F32, name="total")
@@ -157,35 +165,36 @@ def tile_neuromodulatedattentionwithelectrodes_b_kernel(tc, q, k, v, emb, offs, 
             bank = work_banks.tile([P, WB, P], F32, name="flip", tag="work")
             for wb in range(WB):
                 nc.tensor.transpose(bank[:, wb, :], words[:, wb * P : (wb + 1) * P], ident32[:])
-            g, jq = divmod(i, PER_BANK)
+            g, jq = place[i]
             if jq == 0:
-                keys_first[g] = flipped.tile([P, WB, BANK], F32, name="keys_first")
+                keys_first[g] = flipped.tile([P, WB, GROUPS[g][1] * P], F32, name="keys_first")
             nc.scalar.copy(keys_first[g][:, :, jq * P : (jq + 1) * P], bank[:])
 
         acc = {}
 
-        def attend(g, c, h, first=0, count=PER_BANK):
-            s = g // HALVES
-            if h == 0 and first == 0:
-                if g < LAST_GROUP:
+        def attend(g, c, h):
+            first, count = GROUPS[g]
+            s = first // TB
+            if h == 0:
+                if g < WHOLE_GROUPS:
                     acc[g, c] = work_banks.tile([P, BANK], F32, name="acc", tag="work")
                 else:
-                    acc[g, c] = score_banks.tile([P, BANK], F32, name="score")
+                    acc[g, c] = score_banks.tile([P, count * P], F32, name="score")
             halves = keys_first[g][:].rearrange("p b j -> p (b j)").bitcast(BF16)
             halves = halves.rearrange("p (b j e) -> p b j e", b=WB, e=PAIR)
             for t in range(PER_BANK):
                 tb = h * PER_BANK + t
                 nc.tensor.matmul(
-                    acc[g, c][:, first * P : (first + count) * P],
+                    acc[g, c][:],
                     lhsT=values[s, h][:, t, c * P : (c + 1) * P],
-                    rhs=halves[:, tb // PAIR, first * P : (first + count) * P, tb % PAIR],
+                    rhs=halves[:, tb // PAIR, :, tb % PAIR],
                     start=(tb == 0),
                     stop=(tb == TB - 1),
                 )
-            if h == HALVES - 1 and first + count == PER_BANK:
-                result = staged.tile([P, BANK], F32, name="result")
+            if h == HALVES - 1:
+                result = staged.tile([P, count * P], F32, name="result")
                 nc.scalar.copy(result[:], acc[g, c][:])
-                nc.sync.dma_start(out[c * P : (c + 1) * P, g * BANK : (g + 1) * BANK], result[:])
+                nc.sync.dma_start(out[c * P : (c + 1) * P, first * P : (first + count) * P], result[:])
 
         def look_up(name, s, h):
             for c in range(CB):
@@ -202,18 +211,17 @@ def tile_neuromodulatedattentionwithelectrodes_b_kernel(tc, q, k, v, emb, offs, 
                 scores(i)
             if i >= LAG + PER_BANK:
                 g, quarter = divmod(i - LAG - PER_BANK, PER_BANK)
+                attend(g, quarter // HALVES, quarter % HALVES)
+            if i >= LAG:
+                g, quarter = divmod(i - LAG, PER_BANK)
                 if g % HALVES == 0 and quarter < HALVES:
                     look_up("v", g // HALVES, quarter)
-                attend(g, quarter // HALVES, quarter % HALVES)
-            if i == BLOCKS + LAG - 1:
-                for c in range(CB):
-                    for h in range(HALVES):
-                        attend(LAST_GROUP, c, h, 0, PER_BANK - 1)
             if i >= LAG:
                 flip_rows(i - LAG)
             if i < BLOCKS:
                 row_statistics(i)
                 exponentials(i)
-        for c in range(CB):
-            for h in range(HALVES):
-                attend(LAST_GROUP, c, h, PER_BANK - 1, 1)
+        for g in range(WHOLE_GROUPS, len(GROUPS)):
+            for c in range(CB):
+                for h in range(HALVES):
+                    attend(g, c, h)

@@ -85,29 +85,25 @@ def tile_neuromodulatedattentionwithelectrodes_b_kernel(tc, q, k, v, emb, offs, 
                     plain[name, c, s, h][:, n : n + SHORT],
                     ADD,
                 )
-                if name == "q":
+                if name != "v":
                     nc.scalar.copy(rounded[name, c, s, h][:, n : n + SHORT], summed[name, c, s, h][:, n : n + SHORT])
-                if name == "k":
-                    nc.scalar.copy(
-                        rounded[name, c, s, h][:, n : n + SHORT].rearrange("p (w e) -> p w e", e=PAIR),
-                        summed[name, c, s, h][:, n : n + SHORT].rearrange("p (e w) -> p w e", e=PAIR),
-                    )
             if name == "v" and c == CB - 1:
                 flip_values(s, h)
 
         def flip_values(s, h):
             values[s, h] = held.tile([P, PER_BANK, CHANNELS], BF16, name="values%d%d" % (s, h))
-            for pair in range(PER_BANK // 2):
-                bank = work_banks.tile([P, 2, CHANNELS], F32, name="bank", tag="work")
-                for t in range(2):
-                    tb = 2 * pair + t
+            for b in range(PER_BANK // PAIR):
+                bank = work_banks.tile([P, PAIR, CHANNELS], F32, name="bank", tag="work")
+                for e in range(PAIR):
                     for c in range(CB):
                         nc.tensor.transpose(
-                            bank[:, t, c * P : (c + 1) * P], summed["v", c, s, h][:, tb * P : (tb + 1) * P], ident32[:]
+                            bank[:, e, c * P : (c + 1) * P],
+                            summed["v", c, s, h][:, b * SHORT + e : (b + 1) * SHORT : PAIR],
+                            ident32[:],
                         )
-                nc.scalar.copy(values[s, h][:, 2 * pair : 2 * pair + 2, :], bank[:])
+                nc.scalar.copy(values[s, h][:, PAIR * b : PAIR * (b + 1), :], bank[:])
 
-        score, mean_var, deviation, weights, sums = {}, {}, {}, {}, {}
+        score, mean_var, deviation, minus_mean, weights, sums = {}, {}, {}, {}, {}, {}
 
         def scores(i):
             s, jb = divmod(i, TB)
@@ -131,14 +127,16 @@ def tile_neuromodulatedattentionwithelectrodes_b_kernel(tc, q, k, v, emb, offs, 
             nc.vector.bn_aggr(mean_var[i][:], parts[:].rearrange("p h x -> p (h x)"))
             deviation[i] = stats.tile([P, 1], F32, name="deviation")
             nc.gpsimd.tensor_tensor(deviation[i][:], mean_var[i][:, 1:2], half[:], POW)
+            minus_mean[i] = stats.tile([P, 1], F32, name="minus_mean")
+            nc.scalar.mul(minus_mean[i][:], mean_var[i][:, 0:1], -1.0)
 
         def exponentials(i):
             padded = stats.tile([P, 1], F32, name="padded")
-            nc.vector.tensor_scalar(padded[:], deviation[i][:], UNBIAS, SCALE * EPS, MULT, ADD)
+            nc.scalar.activation(padded[:], deviation[i][:], FUNC.Copy, bias=SCALE * EPS, scale=UNBIAS)
             gain = stats.tile([P, 1], F32, name="gain")
             nc.vector.reciprocal(gain[:], padded[:])
             shift = stats.tile([P, 1], F32, name="shift")
-            nc.vector.scalar_tensor_tensor(shift[:], mean_var[i][:, 0:1], -1.0, gain[:], MULT, MULT)
+            nc.scalar.activation(shift[:], gain[:], FUNC.Identity, scale=minus_mean[i][:])
             weights[i] = rows.tile([P, TOKENS], BF16, name="weights")
             sums[i] = stats.tile([P, HALVES], F32, name="sums")
             for h in range(HALVES):

@@ -101,7 +101,8 @@ def tile_neuromodulatedattentionwithelectrodes_b_kernel(tc, q, k, v, emb, offs, 
                             summed["v", c, s, h][:, b * SHORT + e : (b + 1) * SHORT : PAIR],
                             ident32[:],
                         )
-                nc.scalar.copy(values[s, h][:, PAIR * b : PAIR * (b + 1), :], bank[:])
+                for e in range(PAIR):
+                    nc.scalar.copy(values[s, h][:, PAIR * b + e, :], bank[:, e, :])
 
         score, mean_var, deviation, minus_mean, weights, sums = {}, {}, {}, {}, {}, {}
 
@@ -166,7 +167,8 @@ def tile_neuromodulatedattentionwithelectrodes_b_kernel(tc, q, k, v, emb, offs, 
             g, jq = place[i]
             if jq == 0:
                 keys_first[g] = flipped.tile([P, WB, GROUPS[g][1] * P], F32, name="keys_first")
-            nc.scalar.copy(keys_first[g][:, :, jq * P : (jq + 1) * P], bank[:])
+            for wb in range(0, WB, PAIR):
+                nc.scalar.copy(keys_first[g][:, wb : wb + PAIR, jq * P : (jq + 1) * P], bank[:, wb : wb + PAIR, :])
 
         acc = {}
 
@@ -191,7 +193,9 @@ def tile_neuromodulatedattentionwithelectrodes_b_kernel(tc, q, k, v, emb, offs, 
                 )
             if h == HALVES - 1:
                 result = staged.tile([P, count * P], F32, name="result")
-                nc.scalar.copy(result[:], acc[g, c][:])
+                for n in range(0, count * P, SHORT):
+                    end = min(n + SHORT, count * P)
+                    nc.scalar.copy(result[:, n:end], acc[g, c][:, n:end])
                 nc.sync.dma_start(out[c * P : (c + 1) * P, first * P : (first + count) * P], result[:])
 
         def look_up(name, s, h):

@@ -172,17 +172,17 @@ def tile_neuromodulatedattentionwithelectrodes_b_kernel(tc, q, k, v, emb, offs, 
 
         acc = {}
 
-        def attend(g, c, h):
+        def attend(g, c, h, blocks=(0, 1, 2, 3)):
             first, count = GROUPS[g]
             s = first // TB
-            if h == 0:
+            if h == 0 and blocks[0] == 0:
                 if g < WHOLE_GROUPS:
                     acc[g, c] = work_banks.tile([P, BANK], F32, name="acc", tag="work")
                 else:
                     acc[g, c] = score_banks.tile([P, count * P], F32, name="score")
             halves = keys_first[g][:].rearrange("p b j -> p (b j)").bitcast(BF16)
             halves = halves.rearrange("p (b j e) -> p b j e", b=WB, e=PAIR)
-            for t in range(PER_BANK):
+            for t in blocks:
                 tb = h * PER_BANK + t
                 nc.tensor.matmul(
                     acc[g, c][:],
@@ -191,7 +191,7 @@ def tile_neuromodulatedattentionwithelectrodes_b_kernel(tc, q, k, v, emb, offs, 
                     start=(tb == 0),
                     stop=(tb == TB - 1),
                 )
-            if h == HALVES - 1:
+            if h == HALVES - 1 and blocks[-1] == PER_BANK - 1:
                 result = staged.tile([P, count * P], F32, name="result")
                 for n in range(0, count * P, SHORT):
                     end = min(n + SHORT, count * P)
@@ -213,13 +213,16 @@ def tile_neuromodulatedattentionwithelectrodes_b_kernel(tc, q, k, v, emb, offs, 
                 scores(i)
             if i >= LAG + PER_BANK:
                 g, quarter = divmod(i - LAG - PER_BANK, PER_BANK)
-                attend(g, quarter // HALVES, quarter % HALVES)
+                attend(g, quarter // HALVES, quarter % HALVES, (0, 1))
             if i >= LAG:
                 g, quarter = divmod(i - LAG, PER_BANK)
                 if g % HALVES == 0 and quarter < HALVES:
                     look_up("v", g // HALVES, quarter)
             if i >= LAG:
                 flip_rows(i - LAG)
+            if i >= LAG + PER_BANK:
+                g, quarter = divmod(i - LAG - PER_BANK, PER_BANK)
+                attend(g, quarter // HALVES, quarter % HALVES, (2, 3))
             if i < BLOCKS:
                 row_statistics(i)
                 exponentials(i)

@@ -202,15 +202,19 @@ def tile_neuromodulatedattentionwithelectrodes_b_kernel(tc, q, k, v, emb, offs, 
             for c in range(CB):
                 add_embedding(name, c, s, h)
 
-        for i in range(BLOCKS + LAG):
+        def front(i):
             s, jb = divmod(i, TB)
-            if i < BLOCKS:
-                if jb == 0:
-                    for h in range(HALVES):
-                        look_up("k", s, h)
-                if jb % PER_BANK == 0:
-                    look_up("q", s, jb // PER_BANK)
-                scores(i)
+            if jb == 0:
+                for h in range(HALVES):
+                    look_up("k", s, h)
+            if jb % PER_BANK == 0:
+                look_up("q", s, jb // PER_BANK)
+            scores(i)
+
+        front(0)
+        for i in range(BLOCKS + LAG):
+            if i + 1 < BLOCKS:
+                front(i + 1)
             if i >= LAG + PER_BANK:
                 g, quarter = divmod(i - LAG - PER_BANK, PER_BANK)
                 attend(g, quarter // HALVES, quarter % HALVES, (0, 1))

@@ -22,6 +22,9 @@ SCALE = 16.0
 UNBIAS = (TOKENS / (TOKENS - 1.0)) ** 0.5
 GROUPS = ((0, 4), (4, 4), (8, 4), (12, 3), (15, 1))
 WHOLE_GROUPS = 3
+SPARE_FROM = 12
+URGENT_FROM = 15
+AHEAD = 2
 LAG = 2
 
 assert CB * HALVES == PER_BANK
@@ -161,7 +164,10 @@ def tile_neuromodulatedattentionwithelectrodes_b_kernel(tc, q, k, v, emb, offs, 
             softmax = rows.tile([P, TOKENS], BF16, name="softmax")
             nc.vector.tensor_scalar(softmax[:], weights[i][:], inverse[:], None, MULT)
             words = softmax[:].bitcast(F32)
-            bank = work_banks.tile([P, WB, P], F32, name="flip", tag="work")
+            if i < SPARE_FROM:
+                bank = work_banks.tile([P, WB, P], F32, name="flip", tag="work")
+            else:
+                bank = score_banks.tile([P, WB, P], F32, name="score")
             for wb in range(WB):
                 nc.tensor.transpose(bank[:, wb, :], words[:, wb * P : (wb + 1) * P], ident32[:])
             g, jq = place[i]
@@ -176,7 +182,7 @@ def tile_neuromodulatedattentionwithelectrodes_b_kernel(tc, q, k, v, emb, offs, 
             first, count = GROUPS[g]
             s = first // TB
             if h == 0 and blocks[0] == 0:
-                if g < WHOLE_GROUPS:
+                if first + c * HALVES < SPARE_FROM - PER_BANK:
                     acc[g, c] = work_banks.tile([P, BANK], F32, name="acc", tag="work")
                 else:
                     acc[g, c] = score_banks.tile([P, count * P], F32, name="score")
@@ -211,10 +217,14 @@ def tile_neuromodulatedattentionwithelectrodes_b_kernel(tc, q, k, v, emb, offs, 
                 look_up("q", s, jb // PER_BANK)
             scores(i)
 
-        front(0)
+        for i in range(AHEAD):
+            front(i)
         for i in range(BLOCKS + LAG):
-            if i + 1 < BLOCKS:
-                front(i + 1)
+            if i + AHEAD < BLOCKS:
+                front(i + AHEAD)
+            if URGENT_FROM <= i < BLOCKS:
+                row_statistics(i)
+                exponentials(i)
             if i >= LAG + PER_BANK:
                 g, quarter = divmod(i - LAG - PER_BANK, PER_BANK)
                 attend(g, quarter // HALVES, quarter % HALVES, (0, 1))
@@ -227,7 +237,7 @@ def tile_neuromodulatedattentionwithelectrodes_b_kernel(tc, q, k, v, emb, offs, 
             if i >= LAG + PER_BANK:
                 g, quarter = divmod(i - LAG - PER_BANK, PER_BANK)
                 attend(g, quarter // HALVES, quarter % HALVES, (2, 3))
-            if i < BLOCKS:
+            if i < URGENT_FROM:
                 row_statistics(i)
                 exponentials(i)
         for g in range(WHOLE_GROUPS, len(GROUPS)):

@@ -182,7 +182,7 @@ def tile_neuromodulatedattentionwithelectrodes_b_kernel(tc, q, k, v, emb, offs, 
             first, count = GROUPS[g]
             s = first // TB
             if h == 0 and blocks[0] == 0:
-                if first + c * HALVES < SPARE_FROM - PER_BANK:
+                if first + c * HALVES <= SPARE_FROM - PER_BANK:
                     acc[g, c] = work_banks.tile([P, BANK], F32, name="acc", tag="work")
                 else:
                     acc[g, c] = score_banks.tile([P, count * P], F32, name="score")

@@ -20,8 +20,9 @@ BN_STATS_DIM = 6
 EPS = 1e-6
 SCALE = 16.0
 UNBIAS = (TOKENS / (TOKENS - 1.0)) ** 0.5
-GROUPS = ((0, 4), (4, 4), (8, 4), (12, 3), (15, 1))
-WHOLE_GROUPS = 3
+GROUPS = ((0, 4), (4, 4), (8, 3), (11, 3), (14, 2))
+WHOLE_GROUPS = 2
+LATE_GROUPS = 2
 SPARE_FROM = 12
 URGENT_FROM = 15
 AHEAD = 2
@@ -182,8 +183,8 @@ def tile_neuromodulatedattentionwithelectrodes_b_kernel(tc, q, k, v, emb, offs, 
             first, count = GROUPS[g]
             s = first // TB
             if h == 0 and blocks[0] == 0:
-                if first + c * HALVES <= SPARE_FROM - PER_BANK:
-                    acc[g, c] = work_banks.tile([P, BANK], F32, name="acc", tag="work")
+                if g < len(GROUPS) - 1:
+                    acc[g, c] = work_banks.tile([P, count * P], F32, name="acc", tag="work")
                 else:
                     acc[g, c] = score_banks.tile([P, count * P], F32, name="score")
             halves = keys_first[g][:].rearrange("p b j -> p (b j)").bitcast(BF16)
@@ -225,22 +226,27 @@ def tile_neuromodulatedattentionwithelectrodes_b_kernel(tc, q, k, v, emb, offs, 
             if URGENT_FROM <= i < BLOCKS:
                 row_statistics(i)
                 exponentials(i)
-            if i >= LAG + PER_BANK:
+            late = i - (BLOCKS - AHEAD)
+            if LAG + PER_BANK <= i < BLOCKS - AHEAD:
                 g, quarter = divmod(i - LAG - PER_BANK, PER_BANK)
                 attend(g, quarter // HALVES, quarter % HALVES, (0, 1))
+            if late >= 0:
+                attend(WHOLE_GROUPS + late // CB, late % CB, 0)
             if i >= LAG:
                 g, quarter = divmod(i - LAG, PER_BANK)
                 if g % HALVES == 0 and quarter < HALVES:
                     look_up("v", g // HALVES, quarter)
             if i >= LAG:
                 flip_rows(i - LAG)
-            if i >= LAG + PER_BANK:
+            if LAG + PER_BANK <= i < BLOCKS - AHEAD:
                 g, quarter = divmod(i - LAG - PER_BANK, PER_BANK)
                 attend(g, quarter // HALVES, quarter % HALVES, (2, 3))
+            if late >= 0:
+                attend(WHOLE_GROUPS + late // CB, late % CB, 1)
             if i < URGENT_FROM:
                 row_statistics(i)
                 exponentials(i)
-        for g in range(WHOLE_GROUPS, len(GROUPS)):
+        for g in range(WHOLE_GROUPS + LATE_GROUPS, len(GROUPS)):
             for c in range(CB):
                 for h in range(HALVES):
                     attend(g, c, h)

@@ -108,7 +108,7 @@ def tile_neuromodulatedattentionwithelectrodes_b_kernel(tc, q, k, v, emb, offs, 
                 for e in range(PAIR):
                     nc.scalar.copy(values[s, h][:, PAIR * b + e, :], bank[:, e, :])
 
-        score, mean_var, deviation, minus_mean, weights, sums = {}, {}, {}, {}, {}, {}
+        score, parts, mean_var, deviation, minus_mean, weights, sums = {}, {}, {}, {}, {}, {}, {}
 
         def scores(i):
             s, jb = divmod(i, TB)
@@ -124,12 +124,14 @@ def tile_neuromodulatedattentionwithelectrodes_b_kernel(tc, q, k, v, emb, offs, 
                         stop=(c == CB - 1),
                     )
 
-        def row_statistics(i):
-            parts = stats.tile([P, HALVES, BN_STATS_DIM], F32, name="parts")
+        def read_statistics(i):
+            parts[i] = stats.tile([P, HALVES, BN_STATS_DIM], F32, name="parts")
             for h in range(HALVES):
-                nc.vector.bn_stats(parts[:, h, :], score[i, h][:])
+                nc.vector.bn_stats(parts[i][:, h, :], score[i, h][:])
+
+        def join_statistics(i):
             mean_var[i] = stats.tile([P, 2], F32, name="mean_var")
-            nc.vector.bn_aggr(mean_var[i][:], parts[:].rearrange("p h x -> p (h x)"))
+            nc.vector.bn_aggr(mean_var[i][:], parts[i][:].rearrange("p h x -> p (h x)"))
             deviation[i] = stats.tile([P, 1], F32, name="deviation")
             nc.gpsimd.tensor_tensor(deviation[i][:], mean_var[i][:, 1:2], half[:], POW)
             minus_mean[i] = stats.tile([P, 1], F32, name="minus_mean")
@@ -220,11 +222,12 @@ def tile_neuromodulatedattentionwithelectrodes_b_kernel(tc, q, k, v, emb, offs, 
 
         for i in range(AHEAD):
             front(i)
+        read_statistics(0)
         for i in range(BLOCKS + LAG):
             if i + AHEAD < BLOCKS:
                 front(i + AHEAD)
             if URGENT_FROM <= i < BLOCKS:
-                row_statistics(i)
+                join_statistics(i)
                 exponentials(i)
             late = i - (BLOCKS - AHEAD)
             if LAG + PER_BANK <= i < BLOCKS - AHEAD:
@@ -244,7 +247,8 @@ def tile_neuromodulatedattentionwithelectrodes_b_kernel(tc, q, k, v, emb, offs, 
             if late >= 0:
                 attend(WHOLE_GROUPS + late // CB, late % CB, 1)
             if i < URGENT_FROM:
-                row_statistics(i)
+                join_statistics(i)
+                read_statistics(i + 1)
                 exponentials(i)
         for g in range(WHOLE_GROUPS + LATE_GROUPS, len(GROUPS)):
             for c in range(CB):

@@ -124,10 +124,10 @@ def tile_neuromodulatedattentionwithelectrodes_b_kernel(tc, q, k, v, emb, offs, 
                         stop=(c == CB - 1),
                     )
 
-        def read_statistics(i):
-            parts[i] = stats.tile([P, HALVES, BN_STATS_DIM], F32, name="parts")
-            for h in range(HALVES):
-                nc.vector.bn_stats(parts[i][:, h, :], score[i, h][:])
+        def read_statistics(i, h):
+            if h == 0:
+                parts[i] = stats.tile([P, HALVES, BN_STATS_DIM], F32, name="parts")
+            nc.vector.bn_stats(parts[i][:, h, :], score[i, h][:])
 
         def join_statistics(i):
             mean_var[i] = stats.tile([P, 2], F32, name="mean_var")
@@ -222,7 +222,8 @@ def tile_neuromodulatedattentionwithelectrodes_b_kernel(tc, q, k, v, emb, offs, 
 
         for i in range(AHEAD):
             front(i)
-        read_statistics(0)
+        for h in range(HALVES):
+            read_statistics(0, h)
         for i in range(BLOCKS + LAG):
             if i + AHEAD < BLOCKS:
                 front(i + AHEAD)
@@ -248,8 +249,9 @@ def tile_neuromodulatedattentionwithelectrodes_b_kernel(tc, q, k, v, emb, offs, 
                 attend(WHOLE_GROUPS + late // CB, late % CB, 1)
             if i < URGENT_FROM:
                 join_statistics(i)
-                read_statistics(i + 1)
+                read_statistics(i + 1, 0)
                 exponentials(i)
+                read_statistics(i + 1, 1)
         for g in range(WHOLE_GROUPS + LATE_GROUPS, len(GROUPS)):
             for c in range(CB):
                 for h in range(HALVES):

import concourse.mybir as mybir
from concourse.masks import make_identity

F32, BF16, U16 = mybir.dt.float32, mybir.dt.bfloat16, mybir.dt.uint16
ADD, MULT, POW = mybir.AluOpType.add, mybir.AluOpType.mult, mybir.AluOpType.pow
FUNC = mybir.ActivationFunctionType

P = 128
CHANNELS, TABLE_COLS, SAMPLES, TOKENS = 256, 4096, 2, 1024
CB = CHANNELS // P
TB = TOKENS // P
BLOCKS = SAMPLES * TB
BANK = 512
HALVES = TOKENS // BANK
PER_BANK = BANK // P
PAIR = 2
SHORT = PAIR * P
WB = TB // PAIR
BN_STATS_DIM = 6
EPS = 1e-6
SCALE = 16.0
UNBIAS = (TOKENS / (TOKENS - 1.0)) ** 0.5
GROUPS = ((0, 4), (4, 4), (8, 3), (11, 3), (14, 2))
WHOLE_GROUPS = 2
LATE_GROUPS = 2
SPARE_FROM = 12
URGENT_FROM = 15
AHEAD = 2
LAG = 2

assert CB * HALVES == PER_BANK

FLOPS = 2 * 2 * SAMPLES * TOKENS * TOKENS * CHANNELS


def tile_neuromodulatedattentionwithelectrodes_b_kernel(tc, q, k, v, emb, offs, out):
    nc = tc.nc
    with (
        tc.tile_pool(name="held", bufs=1) as held,
        tc.tile_pool(name="stats", bufs=4) as stats,
        tc.tile_pool(name="rows", bufs=4) as rows,
        tc.tile_pool(name="flipped", bufs=3) as flipped,
        tc.tile_pool(name="staged", bufs=4) as staged,
        tc.psum_pool(name="score_banks", bufs=6) as score_banks,
        tc.psum_pool(name="work_banks", bufs=2) as work_banks,
    ):
        ident32 = held.tile([P, P], F32, name="ident32")
        make_identity(nc, ident32[:])
        half = held.tile([P, 1], F32, name="half")
        nc.gpsimd.memset(half[:], 0.5)

        offsets = held.tile([P, SAMPLES * TOKENS // 16], U16, name="offsets")
        nc.sync.dma_start(offsets[:], offs)
        table = [held.tile([P, TABLE_COLS], F32, name="table%d" % c) for c in range(CB)]
        sources = {"q": q, "k": k, "v": v}
        plain = {}

        def load(name, c, s, pieces):
            row = held.tile([P, len(pieces) * BANK], F32, name="%s_plain%d%d%d" % (name, c, s, pieces[0]))
            first = s * TOKENS + pieces[0] * BANK
            nc.sync.dma_start(row[:], sources[name][c * P : (c + 1) * P, first : first + len(pieces) * BANK])
            for n, h in enumerate(pieces):
                plain[name, c, s, h] = row[:, n * BANK : (n + 1) * BANK]

        for c in range(CB):
            nc.sync.dma_start(table[c][:], emb[c * P : (c + 1) * P, :])
            load("k", c, 0, (0,))
            load("k", c, 0, (1,))
            load("q", c, 0, (0,))
        for c in range(CB):
            load("q", c, 0, (1,))
        for name, s in (("v", 0), ("k", 1), ("q", 1), ("v", 1)):
            for c in range(CB):
                load(name, c, s, (0, 1))

        summed = {}
        rounded = {}
        values = {}

        def add_embedding(name, c, s, h):
            summed[name, c, s, h] = held.tile([P, BANK], F32, name="%s_sum%d%d%d" % (name, c, s, h))
            if name != "v":
                rounded[name, c, s, h] = held.tile([P, BANK], BF16, name="%s_bf%d%d%d" % (name, c, s, h))
            for n in range(0, BANK, SHORT):
                first = s * TOKENS + h * BANK + n
                nc.vector.tensor_tensor(
                    summed[name, c, s, h][:, n : n + SHORT],
                    table[c][:].indirect(offsets[:, first // 16 : (first + SHORT) // 16]),
                    plain[name, c, s, h][:, n : n + SHORT],
                    ADD,
                )
                if name != "v":
                    nc.scalar.copy(rounded[name, c, s, h][:, n : n + SHORT], summed[name, c, s, h][:, n : n + SHORT])
            if name == "v" and c == CB - 1:
                flip_values(s, h)

        def flip_values(s, h):
            values[s, h] = held.tile([P, PER_BANK, CHANNELS], BF16, name="values%d%d" % (s, h))
            for b in range(PER_BANK // PAIR):
                bank = work_banks.tile([P, PAIR, CHANNELS], F32, name="bank", tag="work")
                for e in range(PAIR):
                    for c in range(CB):
                        nc.tensor.transpose(
                            bank[:, e, c * P : (c + 1) * P],
                            summed["v", c, s, h][:, b * SHORT + e : (b + 1) * SHORT : PAIR],
                            ident32[:],
                        )
                for e in range(PAIR):
                    nc.scalar.copy(values[s, h][:, PAIR * b + e, :], bank[:, e, :])

        score, parts, mean_var, deviation, minus_mean, weights, sums = {}, {}, {}, {}, {}, {}, {}

        def scores(i):
            s, jb = divmod(i, TB)
            for h in range(HALVES):
                score[i, h] = score_banks.tile([P, BANK], F32, name="score")
            for c in range(CB):
                for h in range(HALVES):
                    nc.tensor.matmul(
                        score[i, h][:],
                        lhsT=rounded["q", c, s, jb // PER_BANK][:, (jb % PER_BANK) * P : (jb % PER_BANK + 1) * P],
                        rhs=rounded["k", c, s, h][:],
                        start=(c == 0),
                        stop=(c == CB - 1),
                    )

        def read_statistics(i, h):
            if h == 0:
                parts[i] = stats.tile([P, HALVES, BN_STATS_DIM], F32, name="parts")
            nc.vector.bn_stats(parts[i][:, h, :], score[i, h][:])

        def join_statistics(i):
            mean_var[i] = stats.tile([P, 2], F32, name="mean_var")
            nc.vector.bn_aggr(mean_var[i][:], parts[i][:].rearrange("p h x -> p (h x)"))
            deviation[i] = stats.tile([P, 1], F32, name="deviation")
            nc.gpsimd.tensor_tensor(deviation[i][:], mean_var[i][:, 1:2], half[:], POW)
            minus_mean[i] = stats.tile([P, 1], F32, name="minus_mean")
            nc.scalar.mul(minus_mean[i][:], mean_var[i][:, 0:1], -1.0)

        def exponentials(i):
            padded = stats.tile([P, 1], F32, name="padded")
            nc.scalar.activation(padded[:], deviation[i][:], FUNC.Copy, bias=SCALE * EPS, scale=UNBIAS)
            gain = stats.tile([P, 1], F32, name="gain")
            nc.vector.reciprocal(gain[:], padded[:])
            shift = stats.tile([P, 1], F32, name="shift")
            nc.scalar.activation(shift[:], gain[:], FUNC.Identity, scale=minus_mean[i][:])
            weights[i] = rows.tile([P, TOKENS], BF16, name="weights")
            sums[i] = stats.tile([P, HALVES], F32, name="sums")
            for h in range(HALVES):
                nc.scalar.activation(
                    weights[i][:, h * BANK : (h + 1) * BANK],
                    score[i, h][:],
                    FUNC.Exp,
                    bias=shift[:],
                    scale=gain[:],
                    accum_out=sums[i][:, h : h + 1],
                )

        keys_first = {}
        place = {first + b: (g, b) for g, (first, count) in enumerate(GROUPS) for b in range(count)}

        def flip_rows(i):
            total = stats.tile([P, 1], F32, name="total")
            nc.vector.tensor_tensor(total[:], sums[i][:, 0:1], sums[i][:, 1:2], ADD)
            inverse = stats.tile([P, 1], F32, name="inverse")
            nc.vector.reciprocal(inverse[:], total[:])
            softmax = rows.tile([P, TOKENS], BF16, name="softmax")
            nc.vector.tensor_scalar(softmax[:], weights[i][:], inverse[:], None, MULT)
            words = softmax[:].bitcast(F32)
            if i < SPARE_FROM:
                bank = work_banks.tile([P, WB, P], F32, name="flip", tag="work")
            else:
                bank = score_banks.tile([P, WB, P], F32, name="score")
            for wb in range(WB):
                nc.tensor.transpose(bank[:, wb, :], words[:, wb * P : (wb + 1) * P], ident32[:])
            g, jq = place[i]
            if jq == 0:
                keys_first[g] = flipped.tile([P, WB, GROUPS[g][1] * P], F32, name="keys_first")
            for wb in range(0, WB, PAIR):
                nc.scalar.copy(keys_first[g][:, wb : wb + PAIR, jq * P : (jq + 1) * P], bank[:, wb : wb + PAIR, :])

        acc = {}

        def attend(g, c, h, blocks=(0, 1, 2, 3)):
            first, count = GROUPS[g]
            s = first // TB
            if h == 0 and blocks[0] == 0:
                if g < len(GROUPS) - 1:
                    acc[g, c] = work_banks.tile([P, count * P], F32, name="acc", tag="work")
                else:
                    acc[g, c] = score_banks.tile([P, count * P], F32, name="score")
            halves = keys_first[g][:].rearrange("p b j -> p (b j)").bitcast(BF16)
            halves = halves.rearrange("p (b j e) -> p b j e", b=WB, e=PAIR)
            for t in blocks:
                tb = h * PER_BANK + t
                nc.tensor.matmul(
                    acc[g, c][:],
                    lhsT=values[s, h][:, t, c * P : (c + 1) * P],
                    rhs=halves[:, tb // PAIR, :, tb % PAIR],
                    start=(tb == 0),
                    stop=(tb == TB - 1),
                )
            if h == HALVES - 1 and blocks[-1] == PER_BANK - 1:
                result = staged.tile([P, count * P], F32, name="result")
                for n in range(0, count * P, SHORT):
                    end = min(n + SHORT, count * P)
                    nc.scalar.copy(result[:, n:end], acc[g, c][:, n:end])
                nc.sync.dma_start(out[c * P : (c + 1) * P, first * P : (first + count) * P], result[:])

        def look_up(name, s, h):
            for c in range(CB):
                add_embedding(name, c, s, h)

        def front(i):
            s, jb = divmod(i, TB)
            if jb == 0:
                for h in range(HALVES):
                    look_up("k", s, h)
            if jb % PER_BANK == 0:
                look_up("q", s, jb // PER_BANK)
            scores(i)

        for i in range(AHEAD):
            front(i)
        for h in range(HALVES):
            read_statistics(0, h)
        for i in range(BLOCKS + LAG):
            if i + AHEAD < BLOCKS:
                front(i + AHEAD)
            if URGENT_FROM <= i < BLOCKS:
                join_statistics(i)
                exponentials(i)
            late = i - (BLOCKS - AHEAD)
            if LAG + PER_BANK <= i < BLOCKS - AHEAD:
                g, quarter = divmod(i - LAG - PER_BANK, PER_BANK)
                attend(g, quarter // HALVES, quarter % HALVES, (0, 1))
            if late >= 0:
                attend(WHOLE_GROUPS + late // CB, late % CB, 0)
            if i >= LAG:
                g, quarter = divmod(i - LAG, PER_BANK)
                if g % HALVES == 0 and quarter < HALVES:
                    look_up("v", g // HALVES, quarter)
            if i >= LAG:
                flip_rows(i - LAG)
            if LAG + PER_BANK <= i < BLOCKS - AHEAD:
                g, quarter = divmod(i - LAG - PER_BANK, PER_BANK)
                attend(g, quarter // HALVES, quarter % HALVES, (2, 3))
            if late >= 0:
                attend(WHOLE_GROUPS + late // CB, late % CB, 1)
            if i < URGENT_FROM:
                join_statistics(i)
                read_statistics(i + 1, 0)
                exponentials(i)
                read_statistics(i + 1, 1)
        for g in range(WHOLE_GROUPS + LATE_GROUPS, len(GROUPS)):
            for c in range(CB):
                for h in range(HALVES):
                    attend(g, c, h)
